import numpy as np
import ml_dtypes


def mxq(x, axis, fmt="e4m3"):
    dtype, down = {"e4m3": (ml_dtypes.float8_e4m3fn, 7), "e5m2": (ml_dtypes.float8_e5m2, 14)}[fmt]
    v = np.moveaxis(np.asarray(x, np.float32).astype(ml_dtypes.bfloat16).astype(np.float64), axis, -1)
    blocks = v.reshape(v.shape[:-1] + (-1, 32))
    amax = np.abs(blocks).max(-1, keepdims=True)
    byte = np.maximum(np.where(amax > 0, np.frexp(amax)[1] - 1 + 127, 0) - down, 1)
    scale = np.exp2(byte - 127.0)
    codes = (blocks / scale).astype(np.float32).astype(dtype).astype(np.float64)
    return np.moveaxis((codes * scale).reshape(v.shape), -1, axis)


WIDE = False


def mx_kscale(k):
    if not WIDE:
        return np.ones(k)
    levels = np.array([10, -10, 5, -5, 0])
    if k % 512:
        return np.exp2(np.random.permutation(np.resize(levels, k // 32))).repeat(32)
    a = np.empty((k // 512, 16))
    for p in range(k // 512):
        a[p, :8] = np.random.permutation(np.resize(levels, 8))
        for g in range(8):
            far = levels[np.abs(levels - a[p, g]) >= 10]
            a[p, g + 8] = far[np.random.randint(len(far))]
    return np.exp2(a.ravel()).repeat(32)


BF16 = ml_dtypes.bfloat16


def bf(x):
    return np.asarray(x, np.float32).astype(BF16)


def f64(x):
    return np.asarray(x).astype(np.float64)


M, N, NFEAT, NHID, NCLASS = 2048, 2048, 512, 512, 8
ADJ_P = 0.01
SIG = 4.5


def setup_inputs():
    s = mx_kscale(NHID)
    t = mx_kscale(NHID)
    c = np.sqrt(2.0 * SIG / np.sqrt(NHID)) / np.sqrt(NHID)
    return {"h": bf(np.maximum(np.random.standard_normal((N, NHID)), 0.0) * s[None, :]),
            "adj": bf(np.random.uniform(size=(N, N)) < ADJ_P),
            "Qw": bf(np.random.standard_normal((NHID, NHID)) * c / s[:, None] * t[None, :]),
            "Qb": bf(np.random.standard_normal(NHID) * 0.1 * t),
            "Kw": bf(np.random.standard_normal((NHID, NHID)) * c / s[:, None] / t[None, :]),
            "Kb": bf(np.random.standard_normal(NHID) * 0.1 / t)}


def reference(h, adj, Qw, Qb, Kw, Kb):
    hq = mxq(f64(h), 1, "e4m3")
    q = (hq @ mxq(f64(Qw), 0, "e4m3")) + f64(Qb)
    k = (hq @ mxq(f64(Kw), 0, "e4m3")) + f64(Kb)
    sc = f64(adj) * (mxq(q, 1, "e4m3") @ mxq(k, 1, "e4m3").T)
    e = np.exp(sc - sc.max(axis=1, keepdims=True))
    return e / e.sum(axis=1, keepdims=True)

@@ -1,0 +1,206 @@
+from contextlib import ExitStack
+
+import concourse.mybir as mybir
+from concourse.masks import make_identity
+
+NODES = 2048
+FEAT = 512
+FLOPS = 2 * 2 * NODES * FEAT * FEAT + 2 * NODES * NODES * FEAT
+
+F32 = mybir.dt.float32
+BF16 = mybir.dt.bfloat16
+U32 = mybir.dt.uint32
+U8 = mybir.dt.uint8
+FP8X4 = mybir.dt.float8_e4m3fn_x4
+ALU = mybir.AluOpType
+ACT = mybir.ActivationFunctionType
+
+BANK_DT = F32
+
+P = 128
+PAIR = 2 * P
+NPAIR = NODES // PAIR
+NROW = NODES // P
+CHUNK = 512
+NCHUNK = NODES // CHUNK
+CAST_ON_SCALAR = 2
+
+
+def tile_gtransformerblock_pb_kernel(tc, h, adj, Qw, Qb, Kw, Kb, out):
+    nc = tc.nc
+    with ExitStack() as ctx:
+        const = ctx.enter_context(tc.tile_pool(name="const", bufs=1))
+        adjp = ctx.enter_context(tc.tile_pool(name="adjp", bufs=1))
+
+        brow = const.tile([P, 2 * FEAT], BF16, name="brow")
+        nc.vector.memset(brow[:], 0.0)
+        nc.scalar.dma_start(out=brow[0:1, 0:FEAT], in_=Kb.rearrange("(o c) -> o c", o=1))
+        nc.scalar.dma_start(out=brow[0:1, FEAT : 2 * FEAT], in_=Qb.rearrange("(o c) -> o c", o=1))
+        ones = const.tile([P, P], BF16, name="ones")
+        nc.vector.memset(ones[:], 1.0)
+        warm = const.tile([P, 1], F32, name="warm")
+        nc.vector.memset(warm[:], 0.0)
+        warm_out = const.tile([P, 1], F32, name="warm_out")
+        nc.scalar.activation(out=warm_out[:], in_=warm[:], func=ACT.Exp)
+        ident = const.tile([P, P], F32, name="ident")
+        make_identity(nc, ident[:])
+
+        bias = {}
+        codes = {}
+        scales = {}
+        for m in ("k", "q"):
+            bias[m] = const.tile([P, FEAT], BF16, name="bias_" + m)
+            codes["w" + m] = const.tile([P, FEAT], U32, name="codes_w" + m, align_bytes=64)
+            scales["w" + m] = const.tile([P, FEAT], U8, name="scales_w" + m, align_bytes=64)
+        for m in ("h", "k", "q"):
+            codes[m] = const.tile([P, NODES], U32, name="codes_" + m, align_bytes=64)
+            scales[m] = const.tile([P, NODES], U8, name="scales_" + m, align_bytes=64)
+
+        with tc.tile_pool(name="head", bufs=1) as head, tc.psum_pool(name="ps_head", bufs=4) as ps_head:
+            w_raw = {}
+            for m, w in (("k", Kw), ("q", Qw)):
+                w_raw[m] = head.tile([P, 4, FEAT], BF16, name="wraw_" + m)
+                nc.sync.dma_start(out=w_raw[m][:], in_=w.rearrange("(p j) c -> p j c", j=4))
+            h_sb = []
+            for g in range(NPAIR):
+                t = head.tile([P, 2, FEAT], BF16, name="h_sb%d" % g)
+                nc.sync.dma_start(out=t[:], in_=h[g * PAIR : (g + 1) * PAIR, :].rearrange("(b p) k -> p b k", p=P))
+                h_sb.append(t)
+            adj_sb = []
+            for i in range(NROW):
+                t = adjp.tile([P, NODES], BF16, name="adj_sb%d" % i)
+                nc.sync.dma_start(out=t[:], in_=adj[i * P : (i + 1) * P, :])
+                adj_sb.append(t)
+
+            for n, m in enumerate(("k", "q")):
+                bp = ps_head.tile([P, FEAT], F32, name="bp_" + m, tag="tr")
+                nc.tensor.matmul(out=bp[:], lhsT=ones[:], rhs=brow[:, n * FEAT : (n + 1) * FEAT], start=True, stop=True)
+                nc.scalar.copy(
+                    out=bias[m][:].rearrange("p (u m e) -> p u m e", u=2, e=2),
+                    in_=bp[:].rearrange("p (m u e) -> p u m e", u=2, e=2),
+                )
+
+            for m in ("k", "q"):
+                wg = head.tile([P, FEAT, 4], BF16, name="wg_" + m, align_bytes=64)
+                src = w_raw[m][:].rearrange("p j (m u e) -> p u m e j", u=2, e=2)
+                for u in range(2):
+                    nc.vector.tensor_copy(
+                        out=wg[:, u * 256 : (u + 1) * 256, :].rearrange("p (m e) j -> p m e j", e=2),
+                        in_=src[:, u],
+                    )
+                nc.vector.quantize_mx(
+                    out=codes["w" + m][:].bitcast(FP8X4),
+                    scales=scales["w" + m][:],
+                    in_=wg[:].rearrange("p c j -> p (c j)"),
+                )
+
+            grouped = {}
+            rounded = {}
+
+            def turn_h(g):
+                words = h_sb[g][:].rearrange("p b k -> p (b k)").bitcast(F32)
+                tr = ps_head.tile([P, 2, 2, P], F32, name="tr_h", tag="tr")
+                for b in range(2):
+                    for u in range(2):
+                        nc.tensor.transpose(tr[:, b, u, :], words[:, 256 * b + u : 256 * (b + 1) : 2], ident[:])
+                hg = head.tile([P, 4 * PAIR], BF16, name="hg", tag="grouped", bufs=6, align_bytes=64)
+                nc.scalar.copy(
+                    out=hg[:].bitcast(F32).rearrange("p (b n u) -> p b n u", b=2, u=2),
+                    in_=tr[:].rearrange("p b u n -> p b n u"),
+                )
+                grouped["h", g] = hg
+
+            def quantize(m, g):
+                cols = slice(g * PAIR, (g + 1) * PAIR)
+                nc.vector.quantize_mx(
+                    out=codes[m][:, cols].bitcast(FP8X4), scales=scales[m][:, cols], in_=grouped[m, g][:]
+                )
+
+            def stage1(g):
+                for b in range(2):
+                    blk = slice(g * PAIR + b * P, g * PAIR + (b + 1) * P)
+                    for m in ("k", "q"):
+                        bank = ps_head.tile([P, FEAT], BANK_DT, name="bank", tag="bank")
+                        nc.tensor.matmul_mx(
+                            out=bank[:],
+                            lhsT=codes["h"][:, blk].bitcast(FP8X4),
+                            lhsT_scale=scales["h"][:, blk],
+                            rhs=codes["w" + m][:].bitcast(FP8X4),
+                            rhs_scale=scales["w" + m][:],
+                            start=True,
+                            stop=True,
+                        )
+                        rd = head.tile([P, FEAT], BF16, name="rd", tag="rounded", bufs=8)
+                        nc.vector.tensor_tensor(out=rd[:], in0=bank[:], in1=bias[m][:], op=ALU.add)
+                        rounded[m, g, b] = rd
+
+            def turn_kq(g):
+                for m in ("k", "q"):
+                    tr = ps_head.tile([P, 2, 2, P], F32, name="tr_kq", tag="tr")
+                    for b in range(2):
+                        words = rounded[m, g, b][:].bitcast(F32)
+                        for u in range(2):
+                            nc.tensor.transpose(tr[:, b, u, :], words[:, P * u : P * (u + 1)], ident[:])
+                    kg = head.tile([P, 4 * PAIR], BF16, name="kg", tag="grouped", bufs=6, align_bytes=64)
+                    nc.scalar.copy(
+                        out=kg[:].bitcast(F32).rearrange("p (b n u) -> p b n u", b=2, u=2),
+                        in_=tr[:].rearrange("p b u n -> p b n u"),
+                    )
+                    grouped[m, g] = kg
+
+            for it in range(NPAIR + 3):
+                if it < NPAIR:
+                    turn_h(it)
+                if 0 <= it - 1 < NPAIR:
+                    quantize("h", it - 1)
+                    stage1(it - 1)
+                if 0 <= it - 2 < NPAIR:
+                    turn_kq(it - 2)
+                if 0 <= it - 3 < NPAIR:
+                    quantize("k", it - 3)
+                    quantize("q", it - 3)
+
+        with tc.tile_pool(name="work", bufs=3) as work, tc.tile_pool(name="small", bufs=6) as small, tc.psum_pool(
+            name="ps_sc", bufs=8
+        ) as ps_sc:
+            for i in range(NROW):
+                rows = slice(i * P, (i + 1) * P)
+                x = work.tile([P, NODES], F32, name="x", tag="x", bufs=4)
+                xb = work.tile([P, NODES], BF16, name="xb", tag="xb", bufs=3)
+                for c in range(NCHUNK):
+                    cs = slice(c * CHUNK, (c + 1) * CHUNK)
+                    sc = ps_sc.tile([P, CHUNK], F32, name="sc", tag="sc")
+                    nc.tensor.matmul_mx(
+                        out=sc[:],
+                        lhsT=codes["q"][:, rows].bitcast(FP8X4),
+                        lhsT_scale=scales["q"][:, rows],
+                        rhs=codes["k"][:, cs].bitcast(FP8X4),
+                        rhs_scale=scales["k"][:, cs],
+                        start=True,
+                        stop=True,
+                    )
+                    nc.vector.tensor_tensor(out=x[:, cs], in0=sc[:], in1=adj_sb[i][:, cs], op=ALU.mult)
+                    if c < CAST_ON_SCALAR:
+                        nc.scalar.copy(out=xb[:, cs], in_=x[:, cs])
+                    else:
+                        nc.gpsimd.tensor_scalar(
+                            out=xb[:, cs], in0=x[:, cs], scalar1=1.0, scalar2=0.0, op0=ALU.mult, op1=ALU.add
+                        )
+                negmax = small.tile([P, 1], F32, name="negmax", tag="negmax")
+                nc.vector.tensor_scalar(
+                    out=xb[:], in0=xb[:], scalar1=-1.0, scalar2=None, op0=ALU.mult, op1=ALU.min, accum_out=negmax[:]
+                )
+                e = work.tile([P, NODES], F32, name="e", tag="e", bufs=4)
+                rowsum = small.tile([P, 1], F32, name="rowsum", tag="rowsum")
+                nc.scalar.activation(out=e[:], in_=x[:], func=ACT.Exp, bias=negmax[:], scale=1.0, accum_out=rowsum[:])
+                recip = small.tile([P, 1], F32, name="recip", tag="recip")
+                nc.vector.reciprocal(out=recip[:], in_=rowsum[:])
+                for hf in range(2):
+                    hs = slice(hf * (NODES // 2), (hf + 1) * (NODES // 2))
+                    if i < NROW - 2:
+                        nc.gpsimd.tensor_scalar(
+                            out=e[:, hs], in0=e[:, hs], scalar1=recip[:], scalar2=0.0, op0=ALU.mult, op1=ALU.add
+                        )
+                    else:
+                        nc.vector.tensor_scalar(out=e[:, hs], in0=e[:, hs], scalar1=recip[:], scalar2=None, op0=ALU.mult)
+                    nc.sync.dma_start(out=out[rows, hs], in_=e[:, hs])

@@ -14,6 +14,7 @@ U8 = mybir.dt.uint8
 FP8X4 = mybir.dt.float8_e4m3fn_x4
 ALU = mybir.AluOpType
 ACT = mybir.ActivationFunctionType
+ENG = mybir.EngineType
 
 BANK_DT = F32
 
@@ -34,8 +35,8 @@ def tile_gtransformerblock_pb_kernel(tc, h, adj, Qw, Qb, Kw, Kb, out):
 
         brow = const.tile([P, 2 * FEAT], BF16, name="brow")
         nc.vector.memset(brow[:], 0.0)
-        nc.scalar.dma_start(out=brow[0:1, 0:FEAT], in_=Kb.rearrange("(o c) -> o c", o=1))
-        nc.scalar.dma_start(out=brow[0:1, FEAT : 2 * FEAT], in_=Qb.rearrange("(o c) -> o c", o=1))
+        nc.sync.dma_start(out=brow[0:1, 0:FEAT], in_=Kb.rearrange("(o c) -> o c", o=1))
+        nc.sync.dma_start(out=brow[0:1, FEAT : 2 * FEAT], in_=Qb.rearrange("(o c) -> o c", o=1))
         ones = const.tile([P, P], BF16, name="ones")
         nc.vector.memset(ones[:], 1.0)
         warm = const.tile([P, 1], F32, name="warm")
@@ -58,14 +59,22 @@ def tile_gtransformerblock_pb_kernel(tc, h, adj, Qw, Qb, Kw, Kb, out):
 
         with tc.tile_pool(name="head", bufs=1) as head, tc.psum_pool(name="ps_head", bufs=4) as ps_head:
             w_raw = {}
-            for m, w in (("k", Kw), ("q", Qw)):
+            h_sb = []
+
+            def load_w(m, w):
                 w_raw[m] = head.tile([P, 4, FEAT], BF16, name="wraw_" + m)
                 nc.sync.dma_start(out=w_raw[m][:], in_=w.rearrange("(p j) c -> p j c", j=4))
-            h_sb = []
-            for g in range(NPAIR):
+
+            def load_h(g):
                 t = head.tile([P, 2, FEAT], BF16, name="h_sb%d" % g)
                 nc.sync.dma_start(out=t[:], in_=h[g * PAIR : (g + 1) * PAIR, :].rearrange("(b p) k -> p b k", p=P))
                 h_sb.append(t)
+
+            load_w("k", Kw)
+            load_h(0)
+            load_w("q", Qw)
+            for g in range(1, NPAIR):
+                load_h(g)
             adj_sb = []
             for i in range(NROW):
                 t = adjp.tile([P, NODES], BF16, name="adj_sb%d" % i)
@@ -84,7 +93,8 @@ def tile_gtransformerblock_pb_kernel(tc, h, adj, Qw, Qb, Kw, Kb, out):
                 wg = head.tile([P, FEAT, 4], BF16, name="wg_" + m, align_bytes=64)
                 src = w_raw[m][:].rearrange("p j (m u e) -> p u m e j", u=2, e=2)
                 for u in range(2):
-                    nc.vector.tensor_copy(
+                    copy = nc.vector.tensor_copy if u == 0 else nc.scalar.copy
+                    copy(
                         out=wg[:, u * 256 : (u + 1) * 256, :].rearrange("p (m e) j -> p m e j", e=2),
                         in_=src[:, u],
                     )
@@ -163,7 +173,14 @@ def tile_gtransformerblock_pb_kernel(tc, h, adj, Qw, Qb, Kw, Kb, out):
         with tc.tile_pool(name="work", bufs=3) as work, tc.tile_pool(name="small", bufs=6) as small, tc.psum_pool(
             name="ps_sc", bufs=8
         ) as ps_sc:
-            for i in range(NROW):
+            x_t = {}
+            xb_t = {}
+            e_t = {}
+            negmax_t = {}
+            rowsum_t = {}
+            recip_t = {}
+
+            def scores(i):
                 rows = slice(i * P, (i + 1) * P)
                 x = work.tile([P, NODES], F32, name="x", tag="x", bufs=4)
                 xb = work.tile([P, NODES], BF16, name="xb", tag="xb", bufs=3)
@@ -186,21 +203,60 @@ def tile_gtransformerblock_pb_kernel(tc, h, adj, Qw, Qb, Kw, Kb, out):
                         nc.gpsimd.tensor_scalar(
                             out=xb[:, cs], in0=x[:, cs], scalar1=1.0, scalar2=0.0, op0=ALU.mult, op1=ALU.add
                         )
+                x_t[i] = x
+                xb_t[i] = xb
+
+            def rowmax(i):
                 negmax = small.tile([P, 1], F32, name="negmax", tag="negmax")
                 nc.vector.tensor_scalar(
-                    out=xb[:], in0=xb[:], scalar1=-1.0, scalar2=None, op0=ALU.mult, op1=ALU.min, accum_out=negmax[:]
+                    out=xb_t[i][:],
+                    in0=xb_t[i][:],
+                    scalar1=-1.0,
+                    scalar2=None,
+                    op0=ALU.mult,
+                    op1=ALU.min,
+                    accum_out=negmax[:],
                 )
+                negmax_t[i] = negmax
+
+            def exponent(i):
                 e = work.tile([P, NODES], F32, name="e", tag="e", bufs=4)
                 rowsum = small.tile([P, 1], F32, name="rowsum", tag="rowsum")
-                nc.scalar.activation(out=e[:], in_=x[:], func=ACT.Exp, bias=negmax[:], scale=1.0, accum_out=rowsum[:])
+                nc.scalar.activation(
+                    out=e[:], in_=x_t[i][:], func=ACT.Exp, bias=negmax_t[i][:], scale=1.0, accum_out=rowsum[:]
+                )
+                e_t[i] = e
+                rowsum_t[i] = rowsum
+
+            def reciprocal(i):
                 recip = small.tile([P, 1], F32, name="recip", tag="recip")
-                nc.vector.reciprocal(out=recip[:], in_=rowsum[:])
+                nc.vector.reciprocal(out=recip[:], in_=rowsum_t[i][:])
+                recip_t[i] = recip
+
+            def normalise(i):
+                rows = slice(i * P, (i + 1) * P)
+                e = e_t[i]
                 for hf in range(2):
                     hs = slice(hf * (NODES // 2), (hf + 1) * (NODES // 2))
-                    if i < NROW - 2:
+                    if not (i % 5 == 2 or i >= NROW - 2):
                         nc.gpsimd.tensor_scalar(
-                            out=e[:, hs], in0=e[:, hs], scalar1=recip[:], scalar2=0.0, op0=ALU.mult, op1=ALU.add
+                            out=e[:, hs], in0=e[:, hs], scalar1=recip_t[i][:], scalar2=0.0, op0=ALU.mult, op1=ALU.add
                         )
                     else:
-                        nc.vector.tensor_scalar(out=e[:, hs], in0=e[:, hs], scalar1=recip[:], scalar2=None, op0=ALU.mult)
+                        nc.vector.tensor_scalar(
+                            out=e[:, hs], in0=e[:, hs], scalar1=recip_t[i][:], scalar2=None, op0=ALU.mult
+                        )
                     nc.sync.dma_start(out=out[rows, hs], in_=e[:, hs])
+
+            with tc.manual_schedule(engines={ENG.DVE, ENG.Activation, ENG.Pool}):
+                for i in range(NROW + 3):
+                    if 0 <= i - 2 < NROW:
+                        exponent(i - 2)
+                    if 0 <= i - 3 < NROW:
+                        normalise(i - 3)
+                    if i < NROW:
+                        scores(i)
+                    if 0 <= i - 1 < NROW:
+                        rowmax(i - 1)
+                    if 0 <= i - 2 < NROW:
+                        reciprocal(i - 2)

from contextlib import ExitStack

import concourse.mybir as mybir
from concourse.masks import make_identity

NODES = 2048
FEAT = 512
FLOPS = 2 * 2 * NODES * FEAT * FEAT + 2 * NODES * NODES * FEAT

F32 = mybir.dt.float32
BF16 = mybir.dt.bfloat16
U32 = mybir.dt.uint32
U8 = mybir.dt.uint8
FP8X4 = mybir.dt.float8_e4m3fn_x4
ALU = mybir.AluOpType
ACT = mybir.ActivationFunctionType
ENG = mybir.EngineType

BANK_DT = F32

P = 128
PAIR = 2 * P
NPAIR = NODES // PAIR
NROW = NODES // P
CHUNK = 512
NCHUNK = NODES // CHUNK
CAST_ON_SCALAR = 2


def tile_gtransformerblock_pb_kernel(tc, h, adj, Qw, Qb, Kw, Kb, out):
    nc = tc.nc
    with ExitStack() as ctx:
        const = ctx.enter_context(tc.tile_pool(name="const", bufs=1))
        adjp = ctx.enter_context(tc.tile_pool(name="adjp", bufs=1))

        brow = const.tile([P, 2 * FEAT], BF16, name="brow")
        nc.vector.memset(brow[:], 0.0)
        nc.sync.dma_start(out=brow[0:1, 0:FEAT], in_=Kb.rearrange("(o c) -> o c", o=1))
        nc.sync.dma_start(out=brow[0:1, FEAT : 2 * FEAT], in_=Qb.rearrange("(o c) -> o c", o=1))
        ones = const.tile([P, P], BF16, name="ones")
        nc.vector.memset(ones[:], 1.0)
        warm = const.tile([P, 1], F32, name="warm")
        nc.vector.memset(warm[:], 0.0)
        warm_out = const.tile([P, 1], F32, name="warm_out")
        nc.scalar.activation(out=warm_out[:], in_=warm[:], func=ACT.Exp)
        ident = const.tile([P, P], F32, name="ident")
        make_identity(nc, ident[:])

        bias = {}
        codes = {}
        scales = {}
        for m in ("k", "q"):
            bias[m] = const.tile([P, FEAT], BF16, name="bias_" + m)
            codes["w" + m] = const.tile([P, FEAT], U32, name="codes_w" + m, align_bytes=64)
            scales["w" + m] = const.tile([P, FEAT], U8, name="scales_w" + m, align_bytes=64)
        for m in ("h", "k", "q"):
            codes[m] = const.tile([P, NODES], U32, name="codes_" + m, align_bytes=64)
            scales[m] = const.tile([P, NODES], U8, name="scales_" + m, align_bytes=64)

        with tc.tile_pool(name="head", bufs=1) as head, tc.psum_pool(name="ps_head", bufs=4) as ps_head:
            w_raw = {}
            h_sb = []

            def load_w(m, w):
                w_raw[m] = head.tile([P, 4, FEAT], BF16, name="wraw_" + m)
                nc.sync.dma_start(out=w_raw[m][:], in_=w.rearrange("(p j) c -> p j c", j=4))

            def load_h(g):
                t = head.tile([P, 2, FEAT], BF16, name="h_sb%d" % g)
                nc.sync.dma_start(out=t[:], in_=h[g * PAIR : (g + 1) * PAIR, :].rearrange("(b p) k -> p b k", p=P))
                h_sb.append(t)

            load_w("k", Kw)
            load_h(0)
            load_w("q", Qw)
            for g in range(1, NPAIR):
                load_h(g)
            adj_sb = []
            for i in range(NROW):
                t = adjp.tile([P, NODES], BF16, name="adj_sb%d" % i)
                nc.sync.dma_start(out=t[:], in_=adj[i * P : (i + 1) * P, :])
                adj_sb.append(t)

            for n, m in enumerate(("k", "q")):
                bp = ps_head.tile([P, FEAT], F32, name="bp_" + m, tag="tr")
                nc.tensor.matmul(out=bp[:], lhsT=ones[:], rhs=brow[:, n * FEAT : (n + 1) * FEAT], start=True, stop=True)
                nc.scalar.copy(
                    out=bias[m][:].rearrange("p (u m e) -> p u m e", u=2, e=2),
                    in_=bp[:].rearrange("p (m u e) -> p u m e", u=2, e=2),
                )

            for m in ("k", "q"):
                wg = head.tile([P, FEAT, 4], BF16, name="wg_" + m, align_bytes=64)
                src = w_raw[m][:].rearrange("p j (m u e) -> p u m e j", u=2, e=2)
                for u in range(2):
                    copy = nc.vector.tensor_copy if u == 0 else nc.scalar.copy
                    copy(
                        out=wg[:, u * 256 : (u + 1) * 256, :].rearrange("p (m e) j -> p m e j", e=2),
                        in_=src[:, u],
                    )
                nc.vector.quantize_mx(
                    out=codes["w" + m][:].bitcast(FP8X4),
                    scales=scales["w" + m][:],
                    in_=wg[:].rearrange("p c j -> p (c j)"),
                )

            grouped = {}
            rounded = {}

            def turn_h(g):
                words = h_sb[g][:].rearrange("p b k -> p (b k)").bitcast(F32)
                tr = ps_head.tile([P, 2, 2, P], F32, name="tr_h", tag="tr")
                for b in range(2):
                    for u in range(2):
                        nc.tensor.transpose(tr[:, b, u, :], words[:, 256 * b + u : 256 * (b + 1) : 2], ident[:])
                hg = head.tile([P, 4 * PAIR], BF16, name="hg", tag="grouped", bufs=6, align_bytes=64)
                nc.scalar.copy(
                    out=hg[:].bitcast(F32).rearrange("p (b n u) -> p b n u", b=2, u=2),
                    in_=tr[:].rearrange("p b u n -> p b n u"),
                )
                grouped["h", g] = hg

            def quantize(m, g):
                cols = slice(g * PAIR, (g + 1) * PAIR)
                nc.vector.quantize_mx(
                    out=codes[m][:, cols].bitcast(FP8X4), scales=scales[m][:, cols], in_=grouped[m, g][:]
                )

            def stage1(g):
                for b in range(2):
                    blk = slice(g * PAIR + b * P, g * PAIR + (b + 1) * P)
                    for m in ("k", "q"):
                        bank = ps_head.tile([P, FEAT], BANK_DT, name="bank", tag="bank")
                        nc.tensor.matmul_mx(
                            out=bank[:],
                            lhsT=codes["h"][:, blk].bitcast(FP8X4),
                            lhsT_scale=scales["h"][:, blk],
                            rhs=codes["w" + m][:].bitcast(FP8X4),
                            rhs_scale=scales["w" + m][:],
                            start=True,
                            stop=True,
                        )
                        rd = head.tile([P, FEAT], BF16, name="rd", tag="rounded", bufs=8)
                        nc.vector.tensor_tensor(out=rd[:], in0=bank[:], in1=bias[m][:], op=ALU.add)
                        rounded[m, g, b] = rd

            def turn_kq(g):
                for m in ("k", "q"):
                    tr = ps_head.tile([P, 2, 2, P], F32, name="tr_kq", tag="tr")
                    for b in range(2):
                        words = rounded[m, g, b][:].bitcast(F32)
                        for u in range(2):
                            nc.tensor.transpose(tr[:, b, u, :], words[:, P * u : P * (u + 1)], ident[:])
                    kg = head.tile([P, 4 * PAIR], BF16, name="kg", tag="grouped", bufs=6, align_bytes=64)
                    nc.scalar.copy(
                        out=kg[:].bitcast(F32).rearrange("p (b n u) -> p b n u", b=2, u=2),
                        in_=tr[:].rearrange("p b u n -> p b n u"),
                    )
                    grouped[m, g] = kg

            for it in range(NPAIR + 3):
                if it < NPAIR:
                    turn_h(it)
                if 0 <= it - 1 < NPAIR:
                    quantize("h", it - 1)
                    stage1(it - 1)
                if 0 <= it - 2 < NPAIR:
                    turn_kq(it - 2)
                if 0 <= it - 3 < NPAIR:
                    quantize("k", it - 3)
                    quantize("q", it - 3)

        with tc.tile_pool(name="work", bufs=3) as work, tc.tile_pool(name="small", bufs=6) as small, tc.psum_pool(
            name="ps_sc", bufs=8
        ) as ps_sc:
            x_t = {}
            xb_t = {}
            e_t = {}
            negmax_t = {}
            rowsum_t = {}
            recip_t = {}

            def scores(i):
                rows = slice(i * P, (i + 1) * P)
                x = work.tile([P, NODES], F32, name="x", tag="x", bufs=4)
                xb = work.tile([P, NODES], BF16, name="xb", tag="xb", bufs=3)
                for c in range(NCHUNK):
                    cs = slice(c * CHUNK, (c + 1) * CHUNK)
                    sc = ps_sc.tile([P, CHUNK], F32, name="sc", tag="sc")
                    nc.tensor.matmul_mx(
                        out=sc[:],
                        lhsT=codes["q"][:, rows].bitcast(FP8X4),
                        lhsT_scale=scales["q"][:, rows],
                        rhs=codes["k"][:, cs].bitcast(FP8X4),
                        rhs_scale=scales["k"][:, cs],
                        start=True,
                        stop=True,
                    )
                    nc.vector.tensor_tensor(out=x[:, cs], in0=sc[:], in1=adj_sb[i][:, cs], op=ALU.mult)
                    if c < CAST_ON_SCALAR:
                        nc.scalar.copy(out=xb[:, cs], in_=x[:, cs])
                    else:
                        nc.gpsimd.tensor_scalar(
                            out=xb[:, cs], in0=x[:, cs], scalar1=1.0, scalar2=0.0, op0=ALU.mult, op1=ALU.add
                        )
                x_t[i] = x
                xb_t[i] = xb

            def rowmax(i):
                negmax = small.tile([P, 1], F32, name="negmax", tag="negmax")
                nc.vector.tensor_scalar(
                    out=xb_t[i][:],
                    in0=xb_t[i][:],
                    scalar1=-1.0,
                    scalar2=None,
                    op0=ALU.mult,
                    op1=ALU.min,
                    accum_out=negmax[:],
                )
                negmax_t[i] = negmax

            def exponent(i):
                e = work.tile([P, NODES], F32, name="e", tag="e", bufs=4)
                rowsum = small.tile([P, 1], F32, name="rowsum", tag="rowsum")
                nc.scalar.activation(
                    out=e[:], in_=x_t[i][:], func=ACT.Exp, bias=negmax_t[i][:], scale=1.0, accum_out=rowsum[:]
                )
                e_t[i] = e
                rowsum_t[i] = rowsum

            def reciprocal(i):
                recip = small.tile([P, 1], F32, name="recip", tag="recip")
                nc.vector.reciprocal(out=recip[:], in_=rowsum_t[i][:])
                recip_t[i] = recip

            def normalise(i):
                rows = slice(i * P, (i + 1) * P)
                e = e_t[i]
                for hf in range(2):
                    hs = slice(hf * (NODES // 2), (hf + 1) * (NODES // 2))
                    if not (i % 5 == 2 or i >= NROW - 2):
                        nc.gpsimd.tensor_scalar(
                            out=e[:, hs], in0=e[:, hs], scalar1=recip_t[i][:], scalar2=0.0, op0=ALU.mult, op1=ALU.add
                        )
                    else:
                        nc.vector.tensor_scalar(
                            out=e[:, hs], in0=e[:, hs], scalar1=recip_t[i][:], scalar2=None, op0=ALU.mult
                        )
                    nc.sync.dma_start(out=out[rows, hs], in_=e[:, hs])

            with tc.manual_schedule(engines={ENG.DVE, ENG.Activation, ENG.Pool}):
                for i in range(NROW + 3):
                    if 0 <= i - 2 < NROW:
                        exponent(i - 2)
                    if 0 <= i - 3 < NROW:
                        normalise(i - 3)
                    if i < NROW:
                        scores(i)
                    if 0 <= i - 1 < NROW:
                        rowmax(i - 1)
                    if 0 <= i - 2 < NROW:
                        reciprocal(i - 2)
